import numpy as np
import ml_dtypes


def mxq(x, axis, fmt="e4m3"):
    dtype, down = {"e4m3": (ml_dtypes.float8_e4m3fn, 7), "e5m2": (ml_dtypes.float8_e5m2, 14)}[fmt]
    v = np.moveaxis(np.asarray(x, np.float32).astype(ml_dtypes.bfloat16).astype(np.float64), axis, -1)
    blocks = v.reshape(v.shape[:-1] + (-1, 32))
    amax = np.abs(blocks).max(-1, keepdims=True)
    byte = np.maximum(np.where(amax > 0, np.frexp(amax)[1] - 1 + 127, 0) - down, 1)
    scale = np.exp2(byte - 127.0)
    codes = (blocks / scale).astype(np.float32).astype(dtype).astype(np.float64)
    return np.moveaxis((codes * scale).reshape(v.shape), -1, axis)


WIDE = False


def mx_kscale(k):
    if not WIDE:
        return np.ones(k)
    levels = np.array([10, -10, 5, -5, 0])
    a = np.random.permutation(np.resize(levels, k // 512 * 4)).reshape(k // 512, 4)
    idx = np.arange(k)
    return np.exp2(a[idx // 512, idx % 128 // 32])


BF16 = ml_dtypes.bfloat16


def bf(x):
    return np.asarray(x, np.float32).astype(BF16)


def f64(x):
    return np.asarray(x).astype(np.float64)


B, U, I = 512, 1024, 512
K = U + I


def sigmoid(v):
    return 1.0 / (1.0 + np.exp(-v))


def setup_inputs():
    s = mx_kscale(K)
    return {"inputs": bf(np.random.standard_normal((B, I)) * s[U:]),
            "h_tm1": bf(np.random.standard_normal((B, U)) * s[:U]),
            "c_tm1": bf(np.random.standard_normal((B, U))),
            "kernel": bf(np.random.standard_normal((K, 4 * U)) / np.sqrt(K) / s[:, None])}


def reference(inputs, h_tm1, c_tm1, kernel):
    a = np.concatenate([f64(h_tm1), f64(inputs)], axis=-1)
    z = mxq(a, 1, "e4m3") @ mxq(f64(kernel), 0, "e4m3")
    z0, z1, z2, z3 = np.split(z, 4, axis=-1)
    i = sigmoid(z0)
    f = sigmoid(z1)
    c_tilde = np.tanh(z2)
    o = sigmoid(z3)
    c = f * f64(c_tm1) + i * c_tilde
    h = o * np.tanh(c)
    return (h, c)

@@ -1,0 +1,193 @@
+from contextlib import ExitStack
+
+import concourse.mybir as mybir
+from concourse.masks import make_identity
+
+F32 = mybir.dt.float32
+BF16 = mybir.dt.bfloat16
+U32 = mybir.dt.uint32
+U8 = mybir.dt.uint8
+FP8X4 = mybir.dt.float8_e4m3fn_x4
+SIGMOID = mybir.ActivationFunctionType.Sigmoid
+TANH = mybir.ActivationFunctionType.Tanh
+
+P = 128
+PACK = 4
+K_PASS = P * PACK
+BATCH, UNITS, FEATURES = 512, 1024, 512
+K = UNITS + FEATURES
+PASSES = K // K_PASS
+BATCH_TILES = BATCH // P
+BANK = 512
+HALVES = UNITS // BANK
+
+GATE_I, GATE_F, GATE_C, GATE_O = 0, 1, 2, 3
+GATE_ORDER = (GATE_F, GATE_I, GATE_C, GATE_O)
+CHUNKS = len(GATE_ORDER) * PASSES
+
+RAW_BUFS = 8
+AHEAD = 2
+VECTOR_COLS = 576
+
+FLOPS = 2 * BATCH * K * 4 * UNITS
+
+
+def tile_customlstmcell_kernel(tc, inputs, h_tm1, c_tm1, kernel, out_0, out_1):
+    nc = tc.nc
+    with ExitStack() as stack:
+        keep = stack.enter_context(tc.tile_pool(name="keep", bufs=1))
+        raw_pool = stack.enter_context(tc.tile_pool(name="raw", bufs=RAW_BUFS))
+        grouped_pool = stack.enter_context(tc.tile_pool(name="grouped", bufs=AHEAD + 2))
+        packed_pool = stack.enter_context(tc.tile_pool(name="packed", bufs=2 * PASSES))
+        gate_pool = stack.enter_context(tc.tile_pool(name="gate", bufs=BATCH_TILES * HALVES))
+        psum = stack.enter_context(tc.psum_pool(name="psum", bufs=8))
+
+        raw_tiles = {}
+
+        def load_chunk(s):
+            gate, c = GATE_ORDER[s // PASSES], s % PASSES
+            raw = raw_pool.tile([P, PACK, UNITS], BF16, name="raw")
+            nc.sync.dma_start(
+                out=raw[:],
+                in_=kernel[
+                    c * K_PASS : (c + 1) * K_PASS, gate * UNITS : (gate + 1) * UNITS
+                ].rearrange("(p j) n -> p j n", j=PACK),
+            )
+            raw_tiles[s] = raw
+
+        a_rows = keep.tile([P, BATCH_TILES * K], BF16)
+        a_rows_by_tile = a_rows[:].rearrange("r (b k) -> r b k", b=BATCH_TILES)
+        c_prev = keep.tile([P, BATCH_TILES, UNITS], BF16)
+
+        load_chunk(0)
+        nc.sync.dma_start(out=a_rows_by_tile[:, :, 0:UNITS], in_=h_tm1.rearrange("(b r) k -> r b k", r=P))
+        nc.sync.dma_start(out=a_rows_by_tile[:, :, UNITS:K], in_=inputs.rearrange("(b r) k -> r b k", r=P))
+        load_chunk(1)
+        load_chunk(2)
+        nc.sync.dma_start(out=c_prev[:], in_=c_tm1.rearrange("(b r) u -> r b u", r=P))
+        for s in range(3, RAW_BUFS):
+            load_chunk(s)
+
+        warm = keep.tile([P, 1], F32)
+        nc.vector.memset(warm[:], 0.0)
+        nc.scalar.activation(out=warm[:], in_=warm[:], func=SIGMOID)
+
+        ident = keep.tile([P, P], F32)
+        make_identity(nc, ident[:])
+
+        grouped_tiles = {}
+        packed_tiles = {}
+
+        def regroup_chunk(s):
+            raw = raw_tiles[s]
+            grouped = grouped_pool.tile([P, UNITS, PACK], BF16, name="grouped", align_bytes=64)
+            for copy, lo, hi in (
+                (nc.vector.tensor_copy, 0, VECTOR_COLS),
+                (nc.scalar.copy, VECTOR_COLS, UNITS),
+            ):
+                copy(
+                    out=grouped[:, lo:hi, :].rearrange("p (n i) t -> p n t i", i=4),
+                    in_=raw[:, :, lo:hi].rearrange("p t (n i) -> p n t i", i=4),
+                )
+            grouped_tiles[s] = grouped
+
+        def quantise_chunk(s):
+            codes = packed_pool.tile([P, UNITS], U32, name="w_codes", align_bytes=64)
+            scales = packed_pool.tile([P, UNITS], U8, name="w_scales", align_bytes=64)
+            nc.vector.quantize_mx(
+                out=codes[:].bitcast(FP8X4),
+                scales=scales[:],
+                in_=grouped_tiles[s][:].rearrange("p n t -> p (n t)"),
+            )
+            packed_tiles[s] = (codes, scales)
+
+        for s in range(AHEAD):
+            regroup_chunk(s)
+
+        a_words = a_rows[:].bitcast(F32)
+        a_grouped = keep.tile([P, PASSES * BATCH * PACK], BF16, align_bytes=64)
+        a_grouped_words = a_grouped[:].bitcast(F32)
+        a_codes = keep.tile([P, PASSES * BATCH], U32, align_bytes=64)
+        a_scales = keep.tile([P, PASSES * BATCH], U8, align_bytes=64)
+        for c in range(PASSES):
+            for pair in range(BATCH_TILES // 2):
+                turned = psum.tile([P, 2, 2, P], F32, tag="bank")
+                for b in range(2):
+                    first = ((2 * pair + b) * K + c * K_PASS) // 2
+                    planes = a_words[:, first : first + K_PASS // 2].rearrange("r (p u) -> r u p", u=2)
+                    for u in range(2):
+                        nc.tensor.transpose(turned[:, b, u, :], planes[:, u, :], ident[:])
+                first = (c * BATCH + 2 * pair * P) * 2
+                nc.scalar.copy(
+                    out=a_grouped_words[:, first : first + 4 * P].rearrange(
+                        "p (b r u) -> p b r u", b=2, u=2
+                    ),
+                    in_=turned[:].rearrange("p b u r -> p b r u"),
+                )
+        for c in range(PASSES):
+            nc.vector.quantize_mx(
+                out=a_codes[:, c * BATCH : (c + 1) * BATCH].bitcast(FP8X4),
+                scales=a_scales[:, c * BATCH : (c + 1) * BATCH],
+                in_=a_grouped[:, c * BATCH * PACK : (c + 1) * BATCH * PACK],
+            )
+
+        banks = [(b, half) for b in range(BATCH_TILES) for half in range(HALVES)]
+        acc = {}
+        cell = {}
+        gate_i = {}
+        tanh_c = {}
+
+        def multiply_chunk(s):
+            c = s % PASSES
+            codes, scales = packed_tiles[s]
+            for b, half in banks:
+                if c == 0:
+                    acc[b, half] = psum.tile([P, BANK], F32, name="acc", tag="bank")
+                rows = slice(c * BATCH + b * P, c * BATCH + (b + 1) * P)
+                cols = slice(half * BANK, (half + 1) * BANK)
+                nc.tensor.matmul_mx(
+                    out=acc[b, half][:],
+                    lhsT=a_codes[:, rows].bitcast(FP8X4),
+                    lhsT_scale=a_scales[:, rows],
+                    rhs=codes[:, cols].bitcast(FP8X4),
+                    rhs_scale=scales[:, cols],
+                    start=(c == 0),
+                    stop=(c == PASSES - 1),
+                )
+
+        def after_gate(gate):
+            for b, half in banks:
+                rows = slice(b * P, (b + 1) * P)
+                cols = slice(half * BANK, (half + 1) * BANK)
+                if gate == GATE_F:
+                    cell[b, half] = gate_pool.tile([P, BANK], F32, name="cell")
+                    nc.scalar.activation(out=cell[b, half][:], in_=acc[b, half][:], func=SIGMOID)
+                    nc.vector.tensor_mul(out=cell[b, half][:], in0=cell[b, half][:], in1=c_prev[:, b, cols])
+                elif gate == GATE_I:
+                    gate_i[b, half] = gate_pool.tile([P, BANK], F32, name="i_then_tanh_c")
+                    nc.scalar.activation(out=gate_i[b, half][:], in_=acc[b, half][:], func=SIGMOID)
+                elif gate == GATE_C:
+                    fresh = gate_pool.tile([P, BANK], F32, name="c_tilde_then_o")
+                    nc.scalar.activation(out=fresh[:], in_=acc[b, half][:], func=TANH)
+                    nc.vector.tensor_mul(out=fresh[:], in0=fresh[:], in1=gate_i[b, half][:])
+                    nc.vector.tensor_add(out=cell[b, half][:], in0=cell[b, half][:], in1=fresh[:])
+                    nc.sync.dma_start(out=out_1[rows, cols], in_=cell[b, half][:])
+                else:
+                    hidden = gate_pool.tile([P, BANK], F32, name="c_tilde_then_o")
+                    nc.scalar.activation(out=hidden[:], in_=acc[b, half][:], func=SIGMOID)
+                    nc.vector.tensor_mul(out=hidden[:], in0=hidden[:], in1=tanh_c[b, half][:])
+                    nc.sync.dma_start(out=out_0[rows, cols], in_=hidden[:])
+            if gate == GATE_C:
+                for b, half in banks:
+                    tanh_c[b, half] = gate_pool.tile([P, BANK], F32, name="i_then_tanh_c")
+                    nc.scalar.activation(out=tanh_c[b, half][:], in_=cell[b, half][:], func=TANH)
+
+        for s in range(CHUNKS):
+            quantise_chunk(s)
+            if s + AHEAD < CHUNKS:
+                regroup_chunk(s + AHEAD)
+            if s + RAW_BUFS < CHUNKS:
+                load_chunk(s + RAW_BUFS)
+            multiply_chunk(s)
+            if s % PASSES == PASSES - 1:
+                after_gate(GATE_ORDER[s // PASSES])

@@ -22,10 +22,10 @@ BANK = 512
 HALVES = UNITS // BANK
 
 GATE_I, GATE_F, GATE_C, GATE_O = 0, 1, 2, 3
-GATE_ORDER = (GATE_F, GATE_I, GATE_C, GATE_O)
+GATE_ORDER = (GATE_I, GATE_C, GATE_F, GATE_O)
 CHUNKS = len(GATE_ORDER) * PASSES
 
-RAW_BUFS = 8
+RAW_BUFS = 6
 AHEAD = 2
 VECTOR_COLS = 576
 
@@ -62,10 +62,7 @@ def tile_customlstmcell_kernel(tc, inputs, h_tm1, c_tm1, kernel, out_0, out_1):
         load_chunk(0)
         nc.sync.dma_start(out=a_rows_by_tile[:, :, 0:UNITS], in_=h_tm1.rearrange("(b r) k -> r b k", r=P))
         nc.sync.dma_start(out=a_rows_by_tile[:, :, UNITS:K], in_=inputs.rearrange("(b r) k -> r b k", r=P))
-        load_chunk(1)
-        load_chunk(2)
-        nc.sync.dma_start(out=c_prev[:], in_=c_tm1.rearrange("(b r) u -> r b u", r=P))
-        for s in range(3, RAW_BUFS):
+        for s in range(1, RAW_BUFS):
             load_chunk(s)
 
         warm = keep.tile([P, 1], F32)
@@ -133,9 +130,6 @@ def tile_customlstmcell_kernel(tc, inputs, h_tm1, c_tm1, kernel, out_0, out_1):
 
         banks = [(b, half) for b in range(BATCH_TILES) for half in range(HALVES)]
         acc = {}
-        cell = {}
-        gate_i = {}
-        tanh_c = {}
 
         def multiply_chunk(s):
             c = s % PASSES
@@ -155,32 +149,15 @@ def tile_customlstmcell_kernel(tc, inputs, h_tm1, c_tm1, kernel, out_0, out_1):
                     stop=(c == PASSES - 1),
                 )
 
-        def after_gate(gate):
+        gate_out = {}
+
+        def activate_gate(gate):
             for b, half in banks:
-                rows = slice(b * P, (b + 1) * P)
-                cols = slice(half * BANK, (half + 1) * BANK)
-                if gate == GATE_F:
-                    cell[b, half] = gate_pool.tile([P, BANK], F32, name="cell")
-                    nc.scalar.activation(out=cell[b, half][:], in_=acc[b, half][:], func=SIGMOID)
-                    nc.vector.tensor_mul(out=cell[b, half][:], in0=cell[b, half][:], in1=c_prev[:, b, cols])
-                elif gate == GATE_I:
-                    gate_i[b, half] = gate_pool.tile([P, BANK], F32, name="i_then_tanh_c")
-                    nc.scalar.activation(out=gate_i[b, half][:], in_=acc[b, half][:], func=SIGMOID)
-                elif gate == GATE_C:
-                    fresh = gate_pool.tile([P, BANK], F32, name="c_tilde_then_o")
-                    nc.scalar.activation(out=fresh[:], in_=acc[b, half][:], func=TANH)
-                    nc.vector.tensor_mul(out=fresh[:], in0=fresh[:], in1=gate_i[b, half][:])
-                    nc.vector.tensor_add(out=cell[b, half][:], in0=cell[b, half][:], in1=fresh[:])
-                    nc.sync.dma_start(out=out_1[rows, cols], in_=cell[b, half][:])
-                else:
-                    hidden = gate_pool.tile([P, BANK], F32, name="c_tilde_then_o")
-                    nc.scalar.activation(out=hidden[:], in_=acc[b, half][:], func=SIGMOID)
-                    nc.vector.tensor_mul(out=hidden[:], in0=hidden[:], in1=tanh_c[b, half][:])
-                    nc.sync.dma_start(out=out_0[rows, cols], in_=hidden[:])
-            if gate == GATE_C:
-                for b, half in banks:
-                    tanh_c[b, half] = gate_pool.tile([P, BANK], F32, name="i_then_tanh_c")
-                    nc.scalar.activation(out=tanh_c[b, half][:], in_=cell[b, half][:], func=TANH)
+                value = gate_pool.tile([P, BANK], F32, name="gate%d" % gate)
+                nc.scalar.activation(
+                    out=value[:], in_=acc[b, half][:], func=TANH if gate == GATE_C else SIGMOID
+                )
+                gate_out[gate, b, half] = value
 
         for s in range(CHUNKS):
             quantise_chunk(s)
@@ -190,4 +167,25 @@ def tile_customlstmcell_kernel(tc, inputs, h_tm1, c_tm1, kernel, out_0, out_1):
                 load_chunk(s + RAW_BUFS)
             multiply_chunk(s)
             if s % PASSES == PASSES - 1:
-                after_gate(GATE_ORDER[s // PASSES])
+                activate_gate(GATE_ORDER[s // PASSES])
+
+        nc.sync.dma_start(out=c_prev[:], in_=c_tm1.rearrange("(b r) u -> r b u", r=P))
+
+        for b, half in banks:
+            fresh = gate_out[GATE_C, b, half]
+            nc.vector.tensor_mul(out=fresh[:], in0=fresh[:], in1=gate_out[GATE_I, b, half][:])
+        for b, half in banks:
+            rows = slice(b * P, (b + 1) * P)
+            cols = slice(half * BANK, (half + 1) * BANK)
+            cell = gate_out[GATE_F, b, half]
+            nc.vector.tensor_mul(out=cell[:], in0=cell[:], in1=c_prev[:, b, cols])
+            nc.vector.tensor_add(out=cell[:], in0=cell[:], in1=gate_out[GATE_C, b, half][:])
+            nc.sync.dma_start(out=out_1[rows, cols], in_=cell[:])
+            tanh_c = gate_out[GATE_I, b, half]
+            nc.scalar.activation(out=tanh_c[:], in_=cell[:], func=TANH)
+        for b, half in banks:
+            rows = slice(b * P, (b + 1) * P)
+            cols = slice(half * BANK, (half + 1) * BANK)
+            hidden = gate_out[GATE_O, b, half]
+            nc.vector.tensor_mul(out=hidden[:], in0=hidden[:], in1=gate_out[GATE_I, b, half][:])
+            nc.sync.dma_start(out=out_0[rows, cols], in_=hidden[:])

@@ -28,6 +28,7 @@ CHUNKS = len(GATE_ORDER) * PASSES
 RAW_BUFS = 6
 AHEAD = 2
 VECTOR_COLS = 576
+RUN = 8
 
 FLOPS = 2 * BATCH * K * 4 * UNITS
 
@@ -83,8 +84,8 @@ def tile_customlstmcell_kernel(tc, inputs, h_tm1, c_tm1, kernel, out_0, out_1):
                 (nc.scalar.copy, VECTOR_COLS, UNITS),
             ):
                 copy(
-                    out=grouped[:, lo:hi, :].rearrange("p (n i) t -> p n t i", i=4),
-                    in_=raw[:, :, lo:hi].rearrange("p t (n i) -> p n t i", i=4),
+                    out=grouped[:, lo:hi, :].rearrange("p (n i) t -> p n t i", i=RUN),
+                    in_=raw[:, :, lo:hi].rearrange("p t (n i) -> p n t i", i=RUN),
                 )
             grouped_tiles[s] = grouped
 

@@ -22,11 +22,11 @@ BANK = 512
 HALVES = UNITS // BANK
 
 GATE_I, GATE_F, GATE_C, GATE_O = 0, 1, 2, 3
-GATE_ORDER = (GATE_I, GATE_C, GATE_F, GATE_O)
-CHUNKS = len(GATE_ORDER) * PASSES
+GATE_ORDER = (GATE_F, GATE_I, GATE_C, GATE_O)
+LOADS = len(GATE_ORDER) * PASSES
 
 RAW_BUFS = 6
-AHEAD = 2
+AHEAD = 4
 VECTOR_COLS = 576
 RUN = 8
 
@@ -38,15 +38,21 @@ def tile_customlstmcell_kernel(tc, inputs, h_tm1, c_tm1, kernel, out_0, out_1):
     with ExitStack() as stack:
         keep = stack.enter_context(tc.tile_pool(name="keep", bufs=1))
         raw_pool = stack.enter_context(tc.tile_pool(name="raw", bufs=RAW_BUFS))
-        grouped_pool = stack.enter_context(tc.tile_pool(name="grouped", bufs=AHEAD + 2))
-        packed_pool = stack.enter_context(tc.tile_pool(name="packed", bufs=2 * PASSES))
+        grouped_pool = stack.enter_context(tc.tile_pool(name="grouped", bufs=AHEAD + 4))
+        packed_pool = stack.enter_context(tc.tile_pool(name="packed", bufs=4 * PASSES))
         gate_pool = stack.enter_context(tc.tile_pool(name="gate", bufs=BATCH_TILES * HALVES))
         psum = stack.enter_context(tc.psum_pool(name="psum", bufs=8))
 
+        chunks = []
+        for whole in range(LOADS):
+            gate, c = GATE_ORDER[whole // PASSES], whole % PASSES
+            chunks.extend([(gate, c, half, 1) for half in range(HALVES)])
+        CHUNKS = len(chunks)
+
         raw_tiles = {}
 
-        def load_chunk(s):
-            gate, c = GATE_ORDER[s // PASSES], s % PASSES
+        def load_kernel(whole):
+            gate, c = GATE_ORDER[whole // PASSES], whole % PASSES
             raw = raw_pool.tile([P, PACK, UNITS], BF16, name="raw")
             nc.sync.dma_start(
                 out=raw[:],
@@ -54,17 +60,18 @@ def tile_customlstmcell_kernel(tc, inputs, h_tm1, c_tm1, kernel, out_0, out_1):
                     c * K_PASS : (c + 1) * K_PASS, gate * UNITS : (gate + 1) * UNITS
                 ].rearrange("(p j) n -> p j n", j=PACK),
             )
-            raw_tiles[s] = raw
+            raw_tiles[whole] = raw
 
         a_rows = keep.tile([P, BATCH_TILES * K], BF16)
         a_rows_by_tile = a_rows[:].rearrange("r (b k) -> r b k", b=BATCH_TILES)
         c_prev = keep.tile([P, BATCH_TILES, UNITS], BF16)
 
-        load_chunk(0)
+        load_kernel(0)
         nc.sync.dma_start(out=a_rows_by_tile[:, :, 0:UNITS], in_=h_tm1.rearrange("(b r) k -> r b k", r=P))
         nc.sync.dma_start(out=a_rows_by_tile[:, :, UNITS:K], in_=inputs.rearrange("(b r) k -> r b k", r=P))
-        for s in range(1, RAW_BUFS):
-            load_chunk(s)
+        for whole in range(1, RAW_BUFS):
+            load_kernel(whole)
+        nc.sync.dma_start(out=c_prev[:], in_=c_tm1.rearrange("(b r) u -> r b u", r=P))
 
         warm = keep.tile([P, 1], F32)
         nc.vector.memset(warm[:], 0.0)
@@ -77,11 +84,13 @@ def tile_customlstmcell_kernel(tc, inputs, h_tm1, c_tm1, kernel, out_0, out_1):
         packed_tiles = {}
 
         def regroup_chunk(s):
-            raw = raw_tiles[s]
-            grouped = grouped_pool.tile([P, UNITS, PACK], BF16, name="grouped", align_bytes=64)
+            first_half, halves = chunks[s][2:]
+            raw = raw_tiles[s // HALVES][:, :, first_half * BANK : (first_half + halves) * BANK]
+            vector_cols = VECTOR_COLS * halves // HALVES
+            grouped = grouped_pool.tile([P, halves * BANK, PACK], BF16, name="grouped", align_bytes=64)
             for copy, lo, hi in (
-                (nc.vector.tensor_copy, 0, VECTOR_COLS),
-                (nc.scalar.copy, VECTOR_COLS, UNITS),
+                (nc.vector.tensor_copy, 0, vector_cols),
+                (nc.scalar.copy, vector_cols, halves * BANK),
             ):
                 copy(
                     out=grouped[:, lo:hi, :].rearrange("p (n i) t -> p n t i", i=RUN),
@@ -90,8 +99,9 @@ def tile_customlstmcell_kernel(tc, inputs, h_tm1, c_tm1, kernel, out_0, out_1):
             grouped_tiles[s] = grouped
 
         def quantise_chunk(s):
-            codes = packed_pool.tile([P, UNITS], U32, name="w_codes", align_bytes=64)
-            scales = packed_pool.tile([P, UNITS], U8, name="w_scales", align_bytes=64)
+            width = chunks[s][3] * BANK
+            codes = packed_pool.tile([P, width], U32, name="w_codes", align_bytes=64)
+            scales = packed_pool.tile([P, width], U8, name="w_scales", align_bytes=64)
             nc.vector.quantize_mx(
                 out=codes[:].bitcast(FP8X4),
                 scales=scales[:],
@@ -133,13 +143,15 @@ def tile_customlstmcell_kernel(tc, inputs, h_tm1, c_tm1, kernel, out_0, out_1):
         acc = {}
 
         def multiply_chunk(s):
-            c = s % PASSES
+            c, first_half, halves = chunks[s][1:]
             codes, scales = packed_tiles[s]
             for b, half in banks:
+                if not first_half <= half < first_half + halves:
+                    continue
                 if c == 0:
                     acc[b, half] = psum.tile([P, BANK], F32, name="acc", tag="bank")
                 rows = slice(c * BATCH + b * P, c * BATCH + (b + 1) * P)
-                cols = slice(half * BANK, (half + 1) * BANK)
+                cols = slice((half - first_half) * BANK, (half - first_half + 1) * BANK)
                 nc.tensor.matmul_mx(
                     out=acc[b, half][:],
                     lhsT=a_codes[:, rows].bitcast(FP8X4),
@@ -164,23 +176,24 @@ def tile_customlstmcell_kernel(tc, inputs, h_tm1, c_tm1, kernel, out_0, out_1):
             quantise_chunk(s)
             if s + AHEAD < CHUNKS:
                 regroup_chunk(s + AHEAD)
-            if s + RAW_BUFS < CHUNKS:
-                load_chunk(s + RAW_BUFS)
+            if s % HALVES == HALVES - 1 and s // HALVES + RAW_BUFS < LOADS:
+                load_kernel(s // HALVES + RAW_BUFS)
             multiply_chunk(s)
-            if s % PASSES == PASSES - 1:
-                activate_gate(GATE_ORDER[s // PASSES])
-
-        nc.sync.dma_start(out=c_prev[:], in_=c_tm1.rearrange("(b r) u -> r b u", r=P))
+            gate, c, first_half, halves = chunks[s]
+            if c == PASSES - 1 and first_half + halves == HALVES:
+                activate_gate(gate)
 
         for b, half in banks:
-            fresh = gate_out[GATE_C, b, half]
-            nc.vector.tensor_mul(out=fresh[:], in0=fresh[:], in1=gate_out[GATE_I, b, half][:])
+            cols = slice(half * BANK, (half + 1) * BANK)
+            cell = gate_out[GATE_F, b, half]
+            nc.vector.tensor_mul(out=cell[:], in0=cell[:], in1=c_prev[:, b, cols])
         for b, half in banks:
             rows = slice(b * P, (b + 1) * P)
             cols = slice(half * BANK, (half + 1) * BANK)
             cell = gate_out[GATE_F, b, half]
-            nc.vector.tensor_mul(out=cell[:], in0=cell[:], in1=c_prev[:, b, cols])
-            nc.vector.tensor_add(out=cell[:], in0=cell[:], in1=gate_out[GATE_C, b, half][:])
+            fresh = gate_out[GATE_C, b, half]
+            nc.vector.tensor_mul(out=fresh[:], in0=fresh[:], in1=gate_out[GATE_I, b, half][:])
+            nc.vector.tensor_add(out=cell[:], in0=cell[:], in1=fresh[:])
             nc.sync.dma_start(out=out_1[rows, cols], in_=cell[:])
             tanh_c = gate_out[GATE_I, b, half]
             nc.scalar.activation(out=tanh_c[:], in_=cell[:], func=TANH)

@@ -26,6 +26,7 @@ GATE_ORDER = (GATE_F, GATE_I, GATE_C, GATE_O)
 LOADS = len(GATE_ORDER) * PASSES
 
 RAW_BUFS = 6
+LOADS_FIRST = 3
 AHEAD = 4
 VECTOR_COLS = 576
 RUN = 8
@@ -66,10 +67,11 @@ def tile_customlstmcell_kernel(tc, inputs, h_tm1, c_tm1, kernel, out_0, out_1):
         a_rows_by_tile = a_rows[:].rearrange("r (b k) -> r b k", b=BATCH_TILES)
         c_prev = keep.tile([P, BATCH_TILES, UNITS], BF16)
 
-        load_kernel(0)
+        for whole in range(LOADS_FIRST):
+            load_kernel(whole)
         nc.sync.dma_start(out=a_rows_by_tile[:, :, 0:UNITS], in_=h_tm1.rearrange("(b r) k -> r b k", r=P))
         nc.sync.dma_start(out=a_rows_by_tile[:, :, UNITS:K], in_=inputs.rearrange("(b r) k -> r b k", r=P))
-        for whole in range(1, RAW_BUFS):
+        for whole in range(LOADS_FIRST, RAW_BUFS):
             load_kernel(whole)
         nc.sync.dma_start(out=c_prev[:], in_=c_tm1.rearrange("(b r) u -> r b u", r=P))
 

from contextlib import ExitStack

import concourse.mybir as mybir
from concourse.masks import make_identity

F32 = mybir.dt.float32
BF16 = mybir.dt.bfloat16
U32 = mybir.dt.uint32
U8 = mybir.dt.uint8
FP8X4 = mybir.dt.float8_e4m3fn_x4
SIGMOID = mybir.ActivationFunctionType.Sigmoid
TANH = mybir.ActivationFunctionType.Tanh

P = 128
PACK = 4
K_PASS = P * PACK
BATCH, UNITS, FEATURES = 512, 1024, 512
K = UNITS + FEATURES
PASSES = K // K_PASS
BATCH_TILES = BATCH // P
BANK = 512
HALVES = UNITS // BANK

GATE_I, GATE_F, GATE_C, GATE_O = 0, 1, 2, 3
GATE_ORDER = (GATE_F, GATE_I, GATE_C, GATE_O)
LOADS = len(GATE_ORDER) * PASSES

RAW_BUFS = 6
LOADS_FIRST = 3
AHEAD = 4
VECTOR_COLS = 576
RUN = 8

FLOPS = 2 * BATCH * K * 4 * UNITS


def tile_customlstmcell_kernel(tc, inputs, h_tm1, c_tm1, kernel, out_0, out_1):
    nc = tc.nc
    with ExitStack() as stack:
        keep = stack.enter_context(tc.tile_pool(name="keep", bufs=1))
        raw_pool = stack.enter_context(tc.tile_pool(name="raw", bufs=RAW_BUFS))
        grouped_pool = stack.enter_context(tc.tile_pool(name="grouped", bufs=AHEAD + 4))
        packed_pool = stack.enter_context(tc.tile_pool(name="packed", bufs=4 * PASSES))
        gate_pool = stack.enter_context(tc.tile_pool(name="gate", bufs=BATCH_TILES * HALVES))
        psum = stack.enter_context(tc.psum_pool(name="psum", bufs=8))

        chunks = []
        for whole in range(LOADS):
            gate, c = GATE_ORDER[whole // PASSES], whole % PASSES
            chunks.extend([(gate, c, half, 1) for half in range(HALVES)])
        CHUNKS = len(chunks)

        raw_tiles = {}

        def load_kernel(whole):
            gate, c = GATE_ORDER[whole // PASSES], whole % PASSES
            raw = raw_pool.tile([P, PACK, UNITS], BF16, name="raw")
            nc.sync.dma_start(
                out=raw[:],
                in_=kernel[
                    c * K_PASS : (c + 1) * K_PASS, gate * UNITS : (gate + 1) * UNITS
                ].rearrange("(p j) n -> p j n", j=PACK),
            )
            raw_tiles[whole] = raw

        a_rows = keep.tile([P, BATCH_TILES * K], BF16)
        a_rows_by_tile = a_rows[:].rearrange("r (b k) -> r b k", b=BATCH_TILES)
        c_prev = keep.tile([P, BATCH_TILES, UNITS], BF16)

        for whole in range(LOADS_FIRST):
            load_kernel(whole)
        nc.sync.dma_start(out=a_rows_by_tile[:, :, 0:UNITS], in_=h_tm1.rearrange("(b r) k -> r b k", r=P))
        nc.sync.dma_start(out=a_rows_by_tile[:, :, UNITS:K], in_=inputs.rearrange("(b r) k -> r b k", r=P))
        for whole in range(LOADS_FIRST, RAW_BUFS):
            load_kernel(whole)
        nc.sync.dma_start(out=c_prev[:], in_=c_tm1.rearrange("(b r) u -> r b u", r=P))

        warm = keep.tile([P, 1], F32)
        nc.vector.memset(warm[:], 0.0)
        nc.scalar.activation(out=warm[:], in_=warm[:], func=SIGMOID)

        ident = keep.tile([P, P], F32)
        make_identity(nc, ident[:])

        grouped_tiles = {}
        packed_tiles = {}

        def regroup_chunk(s):
            first_half, halves = chunks[s][2:]
            raw = raw_tiles[s // HALVES][:, :, first_half * BANK : (first_half + halves) * BANK]
            vector_cols = VECTOR_COLS * halves // HALVES
            grouped = grouped_pool.tile([P, halves * BANK, PACK], BF16, name="grouped", align_bytes=64)
            for copy, lo, hi in (
                (nc.vector.tensor_copy, 0, vector_cols),
                (nc.scalar.copy, vector_cols, halves * BANK),
            ):
                copy(
                    out=grouped[:, lo:hi, :].rearrange("p (n i) t -> p n t i", i=RUN),
                    in_=raw[:, :, lo:hi].rearrange("p t (n i) -> p n t i", i=RUN),
                )
            grouped_tiles[s] = grouped

        def quantise_chunk(s):
            width = chunks[s][3] * BANK
            codes = packed_pool.tile([P, width], U32, name="w_codes", align_bytes=64)
            scales = packed_pool.tile([P, width], U8, name="w_scales", align_bytes=64)
            nc.vector.quantize_mx(
                out=codes[:].bitcast(FP8X4),
                scales=scales[:],
                in_=grouped_tiles[s][:].rearrange("p n t -> p (n t)"),
            )
            packed_tiles[s] = (codes, scales)

        for s in range(AHEAD):
            regroup_chunk(s)

        a_words = a_rows[:].bitcast(F32)
        a_grouped = keep.tile([P, PASSES * BATCH * PACK], BF16, align_bytes=64)
        a_grouped_words = a_grouped[:].bitcast(F32)
        a_codes = keep.tile([P, PASSES * BATCH], U32, align_bytes=64)
        a_scales = keep.tile([P, PASSES * BATCH], U8, align_bytes=64)
        for c in range(PASSES):
            for pair in range(BATCH_TILES // 2):
                turned = psum.tile([P, 2, 2, P], F32, tag="bank")
                for b in range(2):
                    first = ((2 * pair + b) * K + c * K_PASS) // 2
                    planes = a_words[:, first : first + K_PASS // 2].rearrange("r (p u) -> r u p", u=2)
                    for u in range(2):
                        nc.tensor.transpose(turned[:, b, u, :], planes[:, u, :], ident[:])
                first = (c * BATCH + 2 * pair * P) * 2
                nc.scalar.copy(
                    out=a_grouped_words[:, first : first + 4 * P].rearrange(
                        "p (b r u) -> p b r u", b=2, u=2
                    ),
                    in_=turned[:].rearrange("p b u r -> p b r u"),
                )
        for c in range(PASSES):
            nc.vector.quantize_mx(
                out=a_codes[:, c * BATCH : (c + 1) * BATCH].bitcast(FP8X4),
                scales=a_scales[:, c * BATCH : (c + 1) * BATCH],
                in_=a_grouped[:, c * BATCH * PACK : (c + 1) * BATCH * PACK],
            )

        banks = [(b, half) for b in range(BATCH_TILES) for half in range(HALVES)]
        acc = {}

        def multiply_chunk(s):
            c, first_half, halves = chunks[s][1:]
            codes, scales = packed_tiles[s]
            for b, half in banks:
                if not first_half <= half < first_half + halves:
                    continue
                if c == 0:
                    acc[b, half] = psum.tile([P, BANK], F32, name="acc", tag="bank")
                rows = slice(c * BATCH + b * P, c * BATCH + (b + 1) * P)
                cols = slice((half - first_half) * BANK, (half - first_half + 1) * BANK)
                nc.tensor.matmul_mx(
                    out=acc[b, half][:],
                    lhsT=a_codes[:, rows].bitcast(FP8X4),
                    lhsT_scale=a_scales[:, rows],
                    rhs=codes[:, cols].bitcast(FP8X4),
                    rhs_scale=scales[:, cols],
                    start=(c == 0),
                    stop=(c == PASSES - 1),
                )

        gate_out = {}

        def activate_gate(gate):
            for b, half in banks:
                value = gate_pool.tile([P, BANK], F32, name="gate%d" % gate)
                nc.scalar.activation(
                    out=value[:], in_=acc[b, half][:], func=TANH if gate == GATE_C else SIGMOID
                )
                gate_out[gate, b, half] = value

        for s in range(CHUNKS):
            quantise_chunk(s)
            if s + AHEAD < CHUNKS:
                regroup_chunk(s + AHEAD)
            if s % HALVES == HALVES - 1 and s // HALVES + RAW_BUFS < LOADS:
                load_kernel(s // HALVES + RAW_BUFS)
            multiply_chunk(s)
            gate, c, first_half, halves = chunks[s]
            if c == PASSES - 1 and first_half + halves == HALVES:
                activate_gate(gate)

        for b, half in banks:
            cols = slice(half * BANK, (half + 1) * BANK)
            cell = gate_out[GATE_F, b, half]
            nc.vector.tensor_mul(out=cell[:], in0=cell[:], in1=c_prev[:, b, cols])
        for b, half in banks:
            rows = slice(b * P, (b + 1) * P)
            cols = slice(half * BANK, (half + 1) * BANK)
            cell = gate_out[GATE_F, b, half]
            fresh = gate_out[GATE_C, b, half]
            nc.vector.tensor_mul(out=fresh[:], in0=fresh[:], in1=gate_out[GATE_I, b, half][:])
            nc.vector.tensor_add(out=cell[:], in0=cell[:], in1=fresh[:])
            nc.sync.dma_start(out=out_1[rows, cols], in_=cell[:])
            tanh_c = gate_out[GATE_I, b, half]
            nc.scalar.activation(out=tanh_c[:], in_=cell[:], func=TANH)
        for b, half in banks:
            rows = slice(b * P, (b + 1) * P)
            cols = slice(half * BANK, (half + 1) * BANK)
            hidden = gate_out[GATE_O, b, half]
            nc.vector.tensor_mul(out=hidden[:], in0=hidden[:], in1=gate_out[GATE_I, b, half][:])
            nc.sync.dma_start(out=out_0[rows, cols], in_=hidden[:])
